import numpy as np
import ml_dtypes


def mxq(x, axis, fmt="e4m3"):
    dtype, down = {"e4m3": (ml_dtypes.float8_e4m3fn, 7), "e5m2": (ml_dtypes.float8_e5m2, 14)}[fmt]
    v = np.moveaxis(np.asarray(x, np.float32).astype(ml_dtypes.bfloat16).astype(np.float64), axis, -1)
    blocks = v.reshape(v.shape[:-1] + (-1, 32))
    amax = np.abs(blocks).max(-1, keepdims=True)
    byte = np.maximum(np.where(amax > 0, np.frexp(amax)[1] - 1 + 127, 0) - down, 1)
    scale = np.exp2(byte - 127.0)
    codes = (blocks / scale).astype(np.float32).astype(dtype).astype(np.float64)
    return np.moveaxis((codes * scale).reshape(v.shape), -1, axis)


WIDE = False


def mx_kscale(k):
    if not WIDE:
        return np.ones(k)
    levels = np.array([10, -10, 5, -5, 0])
    if k % 512:
        return np.exp2(np.random.permutation(np.resize(levels, k // 32))).repeat(32)
    a = np.empty((k // 512, 16))
    for p in range(k // 512):
        a[p, :8] = np.random.permutation(np.resize(levels, 8))
        for g in range(8):
            far = levels[np.abs(levels - a[p, g]) >= 10]
            a[p, g + 8] = far[np.random.randint(len(far))]
    return np.exp2(a.ravel()).repeat(32)


BF16 = ml_dtypes.bfloat16


def bf(x):
    return np.asarray(x, np.float32).astype(BF16)


def f64(x):
    return np.asarray(x).astype(np.float64)


B, T, L, DM, DC, A, H = 2, 512, 2048, 1024, 512, 512, 4
HD = A // H
ROPE_GAMMA = 10.0


def apply_rope(xh, cos, sin):
    d2 = xh.shape[-1] // 2
    x1, x2 = xh[..., :d2], xh[..., d2:]
    return np.concatenate([x1 * cos - x2 * sin, x1 * sin + x2 * cos], axis=-1)


def prefix_mask(n):
    lens = np.random.randint(n // 2, n, size=B)
    return bf(np.where(np.arange(n)[None, None, :] < lens[:, None, None], 1.0, 0.0))


def draw0():
    s = mx_kscale(DM)
    return {"x": bf(np.random.standard_normal((B, DM, T)) * s[None, :, None]),
            "x_mask": prefix_mask(T),
            "Wq": bf(np.random.standard_normal((A, DM)) * 2.5 / np.sqrt(DM) / s[None, :]),
            "bq": bf(np.random.standard_normal(A) * 0.3)}


def core(x, x_mask, Wq, bq):
    xq = mxq(f64(x), 1, "e4m3")
    q = (xq.transpose(0, 2, 1) @ mxq(f64(Wq), 1, "e4m3").T) + f64(bq)
    q = q.reshape(B, T, H, HD).transpose(2, 0, 1, 3)
    len_q = f64(x_mask).sum(axis=(-2, -1)).reshape(-1, 1, 1)
    pos_q = np.arange(T, dtype=np.float64).reshape(1, -1, 1)
    theta = (ROPE_GAMMA / (10000.0 ** (np.arange(0, HD, 2, dtype=np.float64) / HD))).reshape(1, 1, -1)
    fq = pos_q / len_q * theta
    return apply_rope(q, np.cos(fq)[None], np.sin(fq)[None])


def e4m3fn_bytes(y):
    return np.clip(np.asarray(y, np.float64), -448.0, 448.0).astype(np.float32).astype(ml_dtypes.float8_e4m3fn).view(np.uint8)


def e4m3fn_values(b):
    return np.asarray(b, np.uint8).view(ml_dtypes.float8_e4m3fn).astype(np.float64)


def setup_inputs():
    d = draw0()
    x0 = np.asarray(d['x']).astype(np.float64)
    s = (np.max(np.abs(x0), axis=(0, 2), keepdims=True) / 448.0).astype(np.float32)
    out = {}
    for k, v in d.items():
        if k == 'x':
            out['x_bytes'] = e4m3fn_bytes(x0 / s.astype(np.float64))
            out['x_scale'] = s
        else:
            out[k] = v
    return out


def reference(x_bytes, x_scale, x_mask, Wq, bq):
    return core(e4m3fn_values(x_bytes) * x_scale.astype(np.float64), x_mask, Wq, bq)

@@ -1,0 +1,332 @@
+from contextlib import ExitStack
+
+import concourse.mybir as mybir
+from concourse.masks import make_identity
+
+B, T, DM, A, H = 2, 512, 1024, 512, 4
+HD = A // H
+FLOPS = 2 * B * T * DM * A
+
+F32 = mybir.dt.float32
+BF16 = mybir.dt.bfloat16
+U8 = mybir.dt.uint8
+U32 = mybir.dt.uint32
+I32 = mybir.dt.int32
+FP8 = mybir.dt.float8_e4m3fn
+FP8X4 = mybir.dt.float8_e4m3fn_x4
+ALU = mybir.AluOpType
+ACT = mybir.ActivationFunctionType
+AX = mybir.AxisListType
+
+P = 128
+J = 4
+G = DM // (P * J)
+TB = T // P
+TWO_PI = 6.283185307179586
+
+
+def tile_attentionmodule_pa_kernel(tc, x_bytes, x_scale, x_mask, Wq, bq, out):
+    nc = tc.nc
+    with ExitStack() as ctx:
+        keep = ctx.enter_context(tc.tile_pool(name="keep", bufs=1))
+        work = ctx.enter_context(tc.tile_pool(name="work", bufs=4))
+        ps_q = ctx.enter_context(tc.psum_pool(name="ps_q", bufs=4))
+        ps_t = ctx.enter_context(tc.psum_pool(name="ps_t", bufs=4))
+        ctx.enter_context(tc.manual_schedule())
+
+        xs = keep.tile([P, G, J], F32, name="xs")
+        mk = keep.tile([P, B, 4], BF16, name="mk")
+        zb = keep.tile([P, P], BF16, name="zb")
+        xb, xw, xi, xc, xsc = {}, {}, {}, {}, {}
+        for b in range(B):
+            for g in range(G):
+                xb[(b, g)] = keep.tile([P, J, T], U8, name="xb%d%d" % (b, g))
+                xw[(b, g)] = keep.tile([P, J, T], BF16, name="xw%d%d" % (b, g))
+                xi[(b, g)] = keep.tile([P, T, J], BF16, name="xi%d%d" % (b, g), align_bytes=64)
+                xc[(b, g)] = keep.tile([P, T], U32, name="xc%d%d" % (b, g), align_bytes=64)
+                xsc[(b, g)] = keep.tile([P, T], U8, name="xsc%d%d" % (b, g), align_bytes=64)
+        wraw, wi, wc, wsc = [], [], [], []
+        for r in range(H):
+            wraw.append(keep.tile([P, DM], BF16, name="wraw%d" % r))
+        for rp in range(H // 2):
+            wi.append(keep.tile([P, 2, G * P * J], BF16, name="wi%d" % rp, align_bytes=64))
+            wc.append(keep.tile([P, 2, G * P], U32, name="wc%d" % rp, align_bytes=64))
+            wsc.append(keep.tile([P, 2, G * P], U8, name="wsc%d" % rp, align_bytes=64))
+
+        def load_x(b, g):
+            nc.sync.dma_start(
+                out=xb[(b, g)][:],
+                in_=x_bytes[b].rearrange("(g p j) n -> g p j n", p=P, j=J)[g],
+            )
+
+        def load_w(r):
+            nc.sync.dma_start(out=wraw[r][:], in_=Wq[r * P:(r + 1) * P, :])
+
+        nc.scalar.dma_start(out=mk[:], in_=x_mask.rearrange("b o (p j) -> p (b o) j", j=4))
+        nc.vector.memset(zb[:], 0.0)
+        zero1 = keep.tile([P, 1], F32, name="zero1")
+        nc.vector.memset(zero1[:], 0.0)
+        nc.scalar.dma_start(out=zb[0:H, :], in_=bq.rearrange("(h m) -> h m", m=P))
+        warm = keep.tile([P, 1], F32, name="warm")
+        nc.scalar.activation(out=warm[:], in_=zero1[:], func=ACT.Sin)
+        load_x(0, 0)
+        nc.sync.dma_start(out=xs[:], in_=x_scale.rearrange("o (g p j) q -> p (o g) (j q)", p=P, j=J))
+        load_x(0, 1)
+        load_w(0)
+        load_w(1)
+        load_w(2)
+        load_w(3)
+        load_x(1, 0)
+        load_x(1, 1)
+
+        pidx_i = keep.tile([P, 1], I32, name="pidx_i")
+        nc.gpsimd.iota(pidx_i[:], pattern=[[0, 1]], base=0, channel_multiplier=1)
+        ones = keep.tile([P, P], BF16, name="ones")
+        nc.vector.memset(ones[:], 1.0)
+        pidx = keep.tile([P, 1], F32, name="pidx")
+        nc.vector.tensor_copy(out=pidx[:], in_=pidx_i[:])
+        upper = keep.tile([P, 1], F32, name="upper")
+        nc.vector.tensor_scalar(out=upper[:], in0=pidx[:], scalar1=64.0, scalar2=None, op0=ALU.is_ge)
+        bits = keep.tile([P, 6], I32, name="bits")
+        facs = keep.tile([P, 6], F32, name="facs")
+        for k in range(6):
+            nc.vector.tensor_scalar(out=bits[:, k:k + 1], in0=pidx_i[:], scalar1=k, scalar2=1,
+                                    op0=ALU.logical_shift_right, op1=ALU.bitwise_and)
+        for k in range(6):
+            lead = 10.0 / TWO_PI if k == 0 else 1.0
+            ratio = 10000.0 ** (-(2.0 ** k) / 64.0)
+            nc.vector.tensor_scalar(out=facs[:, k:k + 1], in0=bits[:, k:k + 1], scalar1=(ratio - 1.0) * lead,
+                                    scalar2=lead, op0=ALU.mult, op1=ALU.add)
+        ident = keep.tile([P, P], F32, name="ident")
+        make_identity(nc, ident[:])
+        tpos_i = keep.tile([P, T], I32, name="tpos_i")
+        nc.gpsimd.iota(tpos_i[:], pattern=[[1, T]], base=0, channel_multiplier=0)
+        sgn = keep.tile([P, 1], F32, name="sgn")
+        nc.vector.tensor_scalar(out=sgn[:], in0=upper[:], scalar1=-2.0 * TWO_PI, scalar2=TWO_PI,
+                                op0=ALU.mult, op1=ALU.add)
+        quarter = keep.tile([P, 1], F32, name="quarter")
+        nc.vector.tensor_scalar(out=quarter[:], in0=upper[:], scalar1=0.25, scalar2=None, op0=ALU.mult)
+        turns = keep.tile([P, 1], F32, name="turns")
+        nc.vector.tensor_reduce(out=turns[:], in_=facs[:], axis=AX.X, op=ALU.mult)
+        tpos = keep.tile([P, T], F32, name="tpos")
+        swap = keep.tile([P, P], F32, name="swap")
+        sel_sin = keep.tile([P, P], F32, name="sel_sin")
+        sel_cos = keep.tile([P, P], F32, name="sel_cos")
+        first4 = keep.tile([P, H], BF16, name="first4")
+
+        def selectors():
+            nc.vector.tensor_copy(out=first4[:], in_=ident[:, 0:H])
+            nc.vector.tensor_copy(out=sel_cos[:, 0:64], in_=ident[:, 64:128])
+            nc.vector.tensor_copy(out=sel_cos[:, 64:128], in_=ident[:, 64:128])
+            nc.vector.tensor_copy(out=sel_sin[:, 0:64], in_=ident[:, 0:64])
+            nc.vector.tensor_copy(out=sel_sin[:, 64:128], in_=ident[:, 0:64])
+
+        def swapper():
+            nc.vector.tensor_copy(out=swap[:, 0:64], in_=ident[:, 64:128])
+            nc.vector.tensor_copy(out=swap[:, 64:128], in_=ident[:, 0:64])
+
+        selectors()
+        swapper()
+        nc.vector.tensor_copy(out=tpos[:], in_=tpos_i[:])
+
+        def widen(b, g, j, on_vector):
+            src = xb[(b, g)][:, j, :].bitcast(FP8)
+            dst = xw[(b, g)][:, j, :]
+            if on_vector:
+                nc.vector.tensor_scalar(out=dst, in0=src, scalar1=xs[:, g, j:j + 1], scalar2=None, op0=ALU.mult)
+            else:
+                nc.scalar.activation(out=dst, in_=src, func=ACT.Copy, scale=xs[:, g, j:j + 1])
+
+        def interleave(b, g, on_gpsimd=False, n0=0, n1=T):
+            src = xw[(b, g)][:, :, n0:n1].rearrange("p j (c i) -> p c j i", i=4)
+            dst = xi[(b, g)][:, n0:n1, :].rearrange("p (c i) j -> p c j i", i=4)
+            if on_gpsimd:
+                nc.gpsimd.tensor_scalar(out=dst, in0=src, scalar1=1.0, scalar2=0.0, op0=ALU.mult, op1=ALU.add)
+            else:
+                nc.vector.tensor_copy(out=dst, in_=src)
+
+        def quant_x(b, g):
+            nc.vector.quantize_mx(
+                out=xc[(b, g)][:].bitcast(FP8X4),
+                scales=xsc[(b, g)][:],
+                in_=xi[(b, g)][:].rearrange("p n j -> p (n j)"),
+            )
+
+        wt = {}
+
+        def turn_w(r):
+            words = wraw[r][:].bitcast(F32)
+            wt[r] = ps_t.tile([P, G, 2, P], F32, name="wt%d" % r, tag="tr")
+            for g in range(G):
+                for u in range(2):
+                    nc.tensor.transpose(wt[r][:, g, u, :], words[:, 256 * g + u:256 * (g + 1):2], ident[:])
+
+        def evac_w(r):
+            dst = wi[r // 2][:, r % 2, :].bitcast(F32).rearrange("p (g a u) -> p g a u", g=G, u=2)
+            nc.scalar.copy(out=dst, in_=wt[r][:].rearrange("p g u a -> p g a u"))
+
+        def quant_w(rp):
+            nc.vector.quantize_mx(
+                out=wc[rp][:].rearrange("p r c -> p (r c)").bitcast(FP8X4),
+                scales=wsc[rp][:].rearrange("p r c -> p (r c)"),
+                in_=wi[rp][:].rearrange("p r c -> p (r c)"),
+            )
+
+        step = keep.tile([P, B], F32, name="step")
+        vv, nn, fr, arg, cosT, sinT = {}, {}, {}, {}, {}, {}
+
+        def turns_of(b):
+            vv[b] = keep.tile([P, T], F32, name="vv%d" % b)
+            nc.gpsimd.tensor_scalar(out=vv[b][:], in0=tpos[:], scalar1=step[:, b:b + 1], scalar2=quarter[:, 0:1],
+                                    op0=ALU.mult, op1=ALU.add)
+            nn[b] = keep.tile([P, T], I32, name="nn%d" % b)
+            nc.gpsimd.tensor_scalar(out=nn[b][:], in0=vv[b][:], scalar1=1.0, scalar2=0.0,
+                                    op0=ALU.mult, op1=ALU.add)
+
+        def frac_of(b):
+            fr[b] = keep.tile([P, T], F32, name="fr%d" % b)
+            nc.vector.tensor_tensor(out=fr[b][:], in0=vv[b][:], in1=nn[b][:], op=ALU.subtract)
+
+        def spread(b, which):
+            arg[(b, which)] = ps_t.tile([P, T], F32, name="arg%d%s" % (b, which), tag="tr")
+            sel = sel_cos if which == "c" else sel_sin
+            nc.tensor.matmul(out=arg[(b, which)][:], lhsT=sel[:], rhs=fr[b][:], start=True, stop=True)
+
+        def sine(b, which):
+            tab = keep.tile([P, T], F32, name="tab%d%s" % (b, which))
+            if which == "c":
+                nc.scalar.activation(out=tab[:], in_=arg[(b, which)][:], func=ACT.Sin, scale=TWO_PI)
+                cosT[b] = tab
+            else:
+                nc.scalar.activation(out=tab[:], in_=arg[(b, which)][:], func=ACT.Sin, scale=sgn[:, 0:1])
+                sinT[b] = tab
+
+        bias = keep.tile([P, H], F32, name="bias")
+        qq, pp, ot, ob = {}, {}, {}, {}
+
+        def project(b, h, passes=(0, 1)):
+            if passes[0] == 0:
+                qq[(b, h)] = ps_q.tile([P, T], F32, name="q%d%d" % (b, h), tag="q")
+            for g in passes:
+                cols = slice(g * P, (g + 1) * P)
+                nc.tensor.matmul_mx(
+                    out=qq[(b, h)][:],
+                    lhsT=wc[h // 2][:, h % 2, cols].bitcast(FP8X4),
+                    lhsT_scale=wsc[h // 2][:, h % 2, cols],
+                    rhs=xc[(b, g)][:].bitcast(FP8X4),
+                    rhs_scale=xsc[(b, g)][:],
+                    start=(g == 0),
+                    stop=(g == G - 1),
+                )
+
+        def products(b, h, t0, t1):
+            cols = slice(t0 * P, t1 * P)
+            p1 = work.tile([P, (t1 - t0) * P], F32, name="p1_%d%d%d" % (b, h, t0), tag="p1")
+            nc.vector.scalar_tensor_tensor(out=p1[:], in0=qq[(b, h)][:, cols], scalar=bias[:, h:h + 1],
+                                           in1=cosT[b][:, cols], op0=ALU.add, op1=ALU.mult)
+            p2 = work.tile([P, (t1 - t0) * P], F32, name="p2_%d%d%d" % (b, h, t0), tag="p2")
+            nc.vector.scalar_tensor_tensor(out=p2[:], in0=qq[(b, h)][:, cols], scalar=bias[:, h:h + 1],
+                                           in1=sinT[b][:, cols], op0=ALU.add, op1=ALU.mult)
+            pp[(b, h, t0)] = (p1, p2)
+
+        def turn_out(b, h, t0, t1):
+            p1, p2 = pp[(b, h, t0)]
+            o = ps_t.tile([P, t1 - t0, P], F32, name="ot%d%d%d" % (b, h, t0), tag="tr")
+            for tb in range(t1 - t0):
+                cols = slice(tb * P, (tb + 1) * P)
+                nc.tensor.matmul(out=o[:, tb, :], lhsT=p1[:, cols], rhs=ident[:], is_transpose=True,
+                                 start=True, stop=False)
+                nc.tensor.matmul(out=o[:, tb, :], lhsT=p2[:, cols], rhs=swap[:], is_transpose=True,
+                                 start=False, stop=True)
+            ot[(b, h, t0)] = o
+
+        def evac_out(b, h, t0, t1, on_vector=False, queue=None):
+            o = keep.tile([P, t1 - t0, P], F32, name="ob%d%d%d" % (b, h, t0))
+            if on_vector:
+                nc.vector.tensor_copy(out=o[:], in_=ot[(b, h, t0)][:])
+            else:
+                nc.scalar.copy(out=o[:], in_=ot[(b, h, t0)][:])
+            (queue or nc.sync).dma_start(out=out[h, b].rearrange("(tb p) d -> p tb d", p=P)[:, t0:t1, :], in_=o[:])
+
+        msum = keep.tile([P, B], BF16, name="msum")
+        with nc.allow_low_precision("sums of four ones or zeros are exact in bfloat16"):
+            nc.vector.tensor_reduce(out=msum[:], in_=mk[:], axis=AX.X, op=ALU.add)
+        sm = ps_t.tile([P, 8], F32, name="sm", tag="tr")
+        nc.tensor.matmul(out=sm[:, 0:B], lhsT=ones[:], rhs=msum[:], start=True, stop=True)
+        widen(0, 0, 0, True)
+        widen(0, 0, 2, False)
+        widen(0, 0, 1, True)
+        widen(0, 0, 3, False)
+        rlen = keep.tile([P, B], F32, name="rlen")
+        nc.vector.reciprocal(out=rlen[:], in_=sm[:, 0:B])
+        nc.vector.tensor_scalar(out=step[:], in0=rlen[:], scalar1=turns[:, 0:1], scalar2=None, op0=ALU.mult)
+        turns_of(0)
+        nc.tensor.matmul(out=sm[:, 4:4 + H], lhsT=zb[:], rhs=first4[:], start=True, stop=True)
+        for j in range(J):
+            widen(0, 1, j, False)
+        turn_w(0)
+        turn_w(1)
+        turn_w(2)
+        interleave(0, 0)
+        nc.vector.tensor_copy(out=bias[:], in_=sm[:, 4:4 + H])
+        turn_w(3)
+        frac_of(0)
+        quant_x(0, 0)
+        evac_w(0)
+        evac_w(1)
+        spread(0, "c")
+        spread(0, "s")
+        interleave(0, 1, on_gpsimd=True, n0=0, n1=256)
+        turns_of(1)
+        interleave(0, 1, n0=256, n1=T)
+        evac_w(2)
+        evac_w(3)
+        quant_w(0)
+        quant_x(0, 1)
+        sine(0, "c")
+        sine(0, "s")
+        quant_w(1)
+        for h in range(H):
+            project(0, h)
+        for j in range(J):
+            widen(1, 0, j, False)
+        widen(1, 1, 1, True)
+        products(0, 0, 0, TB)
+        frac_of(1)
+        turn_out(0, 0, 0, TB)
+        spread(1, "c")
+        spread(1, "s")
+        interleave(1, 0, on_gpsimd=True)
+        widen(1, 1, 2, False)
+        widen(1, 1, 3, False)
+        widen(1, 1, 0, True)
+        interleave(1, 1, on_gpsimd=True, n0=0, n1=192)
+        products(0, 1, 0, TB)
+        turn_out(0, 1, 0, TB)
+        sine(1, "c")
+        sine(1, "s")
+        evac_out(0, 0, 0, TB)
+        products(0, 2, 0, TB)
+        turn_out(0, 2, 0, TB)
+        evac_out(0, 1, 0, TB)
+        products(0, 3, 0, TB)
+        turn_out(0, 3, 0, TB)
+        evac_out(0, 2, 0, TB)
+        quant_x(1, 0)
+        for h in range(H):
+            project(1, h, (0,))
+        interleave(1, 1, n0=192, n1=T)
+        evac_out(0, 3, 0, TB)
+        quant_x(1, 1)
+        for h in range(H):
+            project(1, h, (1,))
+        for h in range(H - 1):
+            products(1, h, 0, TB)
+            turn_out(1, h, 0, TB)
+            evac_out(1, h, 0, TB)
+        products(1, 3, 0, 2)
+        turn_out(1, 3, 0, 2)
+        evac_out(1, 3, 0, 2)
+        products(1, 3, 2, 4)
+        turn_out(1, 3, 2, 4)
+        evac_out(1, 3, 2, 4, queue=nc.scalar)

@@ -106,6 +106,8 @@ def tile_attentionmodule_pa_kernel(tc, x_bytes, x_scale, x_mask, Wq, bq, out):
                                 op0=ALU.mult, op1=ALU.add)
         quarter = keep.tile([P, 1], F32, name="quarter")
         nc.vector.tensor_scalar(out=quarter[:], in0=upper[:], scalar1=0.25, scalar2=None, op0=ALU.mult)
+        halfpi = keep.tile([P, 1], F32, name="halfpi")
+        nc.vector.tensor_scalar(out=halfpi[:], in0=upper[:], scalar1=0.0, scalar2=TWO_PI / 4.0, op0=ALU.mult, op1=ALU.add)
         turns = keep.tile([P, 1], F32, name="turns")
         nc.vector.tensor_reduce(out=turns[:], in_=facs[:], axis=AX.X, op=ALU.mult)
         tpos = keep.tile([P, T], F32, name="tpos")
@@ -137,12 +139,15 @@ def tile_attentionmodule_pa_kernel(tc, x_bytes, x_scale, x_mask, Wq, bq, out):
             else:
                 nc.scalar.activation(out=dst, in_=src, func=ACT.Copy, scale=xs[:, g, j:j + 1])
 
-        def interleave(b, g, on_gpsimd=False, n0=0, n1=T):
-            src = xw[(b, g)][:, :, n0:n1].rearrange("p j (c i) -> p c j i", i=4)
-            dst = xi[(b, g)][:, n0:n1, :].rearrange("p (c i) j -> p c j i", i=4)
-            if on_gpsimd:
-                nc.gpsimd.tensor_scalar(out=dst, in0=src, scalar1=1.0, scalar2=0.0, op0=ALU.mult, op1=ALU.add)
+        def interleave(b, g, on_gpsimd=False, n0=0, n1=T, on_scalar=False):
+            if on_scalar:
+                nc.scalar.copy(out=xi[(b, g)][:, n0:n1, :], in_=xw[(b, g)][:, :, n0:n1].rearrange("p j n -> p n j"))
+            elif on_gpsimd:
+                nc.gpsimd.tensor_scalar(out=xi[(b, g)][:, n0:n1, :], in0=xw[(b, g)][:, :, n0:n1].rearrange("p j n -> p n j"),
+                                        scalar1=1.0, scalar2=0.0, op0=ALU.mult, op1=ALU.add)
             else:
+                src = xw[(b, g)][:, :, n0:n1].rearrange("p j (c i) -> p c j i", i=4)
+                dst = xi[(b, g)][:, n0:n1, :].rearrange("p (c i) j -> p c j i", i=4)
                 nc.vector.tensor_copy(out=dst, in_=src)
 
         def quant_x(b, g):
@@ -187,6 +192,22 @@ def tile_attentionmodule_pa_kernel(tc, x_bytes, x_scale, x_mask, Wq, bq, out):
             fr[b] = keep.tile([P, T], F32, name="fr%d" % b)
             nc.vector.tensor_tensor(out=fr[b][:], in0=vv[b][:], in1=nn[b][:], op=ALU.subtract)
 
+        def whole_turns(b):
+            nn[b] = keep.tile([P, T], I32, name="nn%d" % b)
+            nc.vector.tensor_scalar(out=nn[b][:], in0=tpos[:], scalar1=step[:, b:b + 1], scalar2=quarter[:, 0:1],
+                                    op0=ALU.mult, op1=ALU.add)
+
+        def rest_turns(b):
+            fr[b] = keep.tile([P, T], F32, name="fr%d" % b)
+            nc.vector.scalar_tensor_tensor(out=fr[b][:], in0=tpos[:], scalar=step[:, b:b + 1], in1=nn[b][:],
+                                           op0=ALU.mult, op1=ALU.subtract)
+
+        def dup(b):
+            for which, lo in (("s", 0), ("c", 64)):
+                arg[(b, which)] = keep.tile([P, T], F32, name="arg%d%s" % (b, which))
+                nc.sync.dma_start(out=arg[(b, which)][0:64, :], in_=fr[b][lo:lo + 64, :])
+                nc.sync.dma_start(out=arg[(b, which)][64:128, :], in_=fr[b][lo:lo + 64, :])
+
         def spread(b, which):
             arg[(b, which)] = ps_t.tile([P, T], F32, name="arg%d%s" % (b, which), tag="tr")
             sel = sel_cos if which == "c" else sel_sin
@@ -195,7 +216,7 @@ def tile_attentionmodule_pa_kernel(tc, x_bytes, x_scale, x_mask, Wq, bq, out):
         def sine(b, which):
             tab = keep.tile([P, T], F32, name="tab%d%s" % (b, which))
             if which == "c":
-                nc.scalar.activation(out=tab[:], in_=arg[(b, which)][:], func=ACT.Sin, scale=TWO_PI)
+                nc.scalar.activation(out=tab[:], in_=arg[(b, which)][:], func=ACT.Sin, scale=TWO_PI, bias=halfpi[:, 0:1])
                 cosT[b] = tab
             else:
                 nc.scalar.activation(out=tab[:], in_=arg[(b, which)][:], func=ACT.Sin, scale=sgn[:, 0:1])
@@ -253,73 +274,73 @@ def tile_attentionmodule_pa_kernel(tc, x_bytes, x_scale, x_mask, Wq, bq, out):
             nc.vector.tensor_reduce(out=msum[:], in_=mk[:], axis=AX.X, op=ALU.add)
         sm = ps_t.tile([P, 8], F32, name="sm", tag="tr")
         nc.tensor.matmul(out=sm[:, 0:B], lhsT=ones[:], rhs=msum[:], start=True, stop=True)
+        rlen = keep.tile([P, B], F32, name="rlen")
         widen(0, 0, 0, True)
         widen(0, 0, 2, False)
+        nc.vector.reciprocal(out=rlen[:], in_=sm[:, 0:B])
         widen(0, 0, 1, True)
         widen(0, 0, 3, False)
-        rlen = keep.tile([P, B], F32, name="rlen")
-        nc.vector.reciprocal(out=rlen[:], in_=sm[:, 0:B])
         nc.vector.tensor_scalar(out=step[:], in0=rlen[:], scalar1=turns[:, 0:1], scalar2=None, op0=ALU.mult)
-        turns_of(0)
+        widen(0, 1, 0, True)
+        widen(0, 1, 2, False)
+        whole_turns(0)
+        widen(0, 1, 1, True)
+        widen(0, 1, 3, False)
+        rest_turns(0)
+        dup(0)
         nc.tensor.matmul(out=sm[:, 4:4 + H], lhsT=zb[:], rhs=first4[:], start=True, stop=True)
-        for j in range(J):
-            widen(0, 1, j, False)
         turn_w(0)
         turn_w(1)
         turn_w(2)
         interleave(0, 0)
         nc.vector.tensor_copy(out=bias[:], in_=sm[:, 4:4 + H])
         turn_w(3)
-        frac_of(0)
-        quant_x(0, 0)
+        whole_turns(1)
         evac_w(0)
         evac_w(1)
-        spread(0, "c")
-        spread(0, "s")
-        interleave(0, 1, on_gpsimd=True, n0=0, n1=256)
-        turns_of(1)
-        interleave(0, 1, n0=256, n1=T)
+        widen(1, 0, 0, False)
+        interleave(0, 1)
         evac_w(2)
+        widen(1, 0, 1, False)
+        quant_x(0, 0)
         evac_w(3)
         quant_w(0)
+        project(0, 0, (0,))
+        project(0, 1, (0,))
         quant_x(0, 1)
+        project(0, 0, (1,))
+        project(0, 1, (1,))
         sine(0, "c")
         sine(0, "s")
+        rest_turns(1)
+        dup(1)
         quant_w(1)
-        for h in range(H):
-            project(0, h)
-        for j in range(J):
-            widen(1, 0, j, False)
-        widen(1, 1, 1, True)
-        products(0, 0, 0, TB)
-        frac_of(1)
-        turn_out(0, 0, 0, TB)
-        spread(1, "c")
-        spread(1, "s")
+        project(0, 2)
+        project(0, 3)
+        widen(1, 0, 2, False)
+        widen(1, 0, 3, False)
         interleave(1, 0, on_gpsimd=True)
-        widen(1, 1, 2, False)
-        widen(1, 1, 3, False)
-        widen(1, 1, 0, True)
-        interleave(1, 1, on_gpsimd=True, n0=0, n1=192)
-        products(0, 1, 0, TB)
-        turn_out(0, 1, 0, TB)
+        for j in range(J):
+            widen(1, 1, j, False)
+        interleave(1, 1, on_scalar=True, n0=0, n1=320)
+        for h in range(H - 1):
+            products(0, h, 0, TB)
+            turn_out(0, h, 0, TB)
         sine(1, "c")
         sine(1, "s")
-        evac_out(0, 0, 0, TB)
-        products(0, 2, 0, TB)
-        turn_out(0, 2, 0, TB)
-        evac_out(0, 1, 0, TB)
+        quant_x(1, 0)
+        project(1, 0, (0,))
+        interleave(1, 1, n0=320, n1=T)
+        for h in range(H - 1):
+            evac_out(0, h, 0, TB)
+        quant_x(1, 1)
+        project(1, 0, (1,))
+        project(1, 1)
+        project(1, 2)
         products(0, 3, 0, TB)
         turn_out(0, 3, 0, TB)
-        evac_out(0, 2, 0, TB)
-        quant_x(1, 0)
-        for h in range(H):
-            project(1, h, (0,))
-        interleave(1, 1, n0=192, n1=T)
         evac_out(0, 3, 0, TB)
-        quant_x(1, 1)
-        for h in range(H):
-            project(1, h, (1,))
+        project(1, 3)
         for h in range(H - 1):
             products(1, h, 0, TB)
             turn_out(1, h, 0, TB)

@@ -30,7 +30,7 @@ def tile_attentionmodule_pa_kernel(tc, x_bytes, x_scale, x_mask, Wq, bq, out):
     with ExitStack() as ctx:
         keep = ctx.enter_context(tc.tile_pool(name="keep", bufs=1))
         work = ctx.enter_context(tc.tile_pool(name="work", bufs=4))
-        ps_q = ctx.enter_context(tc.psum_pool(name="ps_q", bufs=4))
+        ps_q = ctx.enter_context(tc.psum_pool(name="ps_q", bufs=1))
         ps_t = ctx.enter_context(tc.psum_pool(name="ps_t", bufs=4))
         ctx.enter_context(tc.manual_schedule())
 
@@ -225,9 +225,9 @@ def tile_attentionmodule_pa_kernel(tc, x_bytes, x_scale, x_mask, Wq, bq, out):
         bias = keep.tile([P, H], F32, name="bias")
         qq, pp, ot, ob = {}, {}, {}, {}
 
-        def project(b, h, passes=(0, 1)):
+        def project(b, h, passes=(0, 1), bank=None):
             if passes[0] == 0:
-                qq[(b, h)] = ps_q.tile([P, T], F32, name="q%d%d" % (b, h), tag="q")
+                qq[(b, h)] = ps_q.tile([P, T], F32, name="q%d%d" % (b, h), tag="q%d" % (h if bank is None else bank))
             for g in passes:
                 cols = slice(g * P, (g + 1) * P)
                 nc.tensor.matmul_mx(
@@ -249,6 +249,31 @@ def tile_attentionmodule_pa_kernel(tc, x_bytes, x_scale, x_mask, Wq, bq, out):
             nc.vector.scalar_tensor_tensor(out=p2[:], in0=qq[(b, h)][:, cols], scalar=bias[:, h:h + 1],
                                            in1=sinT[b][:, cols], op0=ALU.add, op1=ALU.mult)
             pp[(b, h, t0)] = (p1, p2)
+
+        qb = {}
+
+        def evac_q(b, h):
+            qb[(b, h)] = keep.tile([P, T], F32, name="qb%d%d" % (b, h))
+            nc.scalar.activation(out=qb[(b, h)][:], in_=qq[(b, h)][:], func=ACT.Identity, bias=bias[:, h:h + 1])
+
+        def products_g(b, h, t0, t1):
+            cols = slice(t0 * P, t1 * P)
+            p1 = keep.tile([P, (t1 - t0) * P], F32, name="p1_%d%d%d" % (b, h, t0))
+            nc.gpsimd.tensor_tensor(out=p1[:], in0=qb[(b, h)][:, cols], in1=cosT[b][:, cols], op=ALU.mult)
+            p2 = keep.tile([P, (t1 - t0) * P], F32, name="p2_%d%d%d" % (b, h, t0))
+            nc.gpsimd.tensor_tensor(out=p2[:], in0=qb[(b, h)][:, cols], in1=sinT[b][:, cols], op=ALU.mult)
+            pp[(b, h, t0)] = (p1, p2)
+
+        def product(b, h, which, on_gpsimd=False):
+            tab = cosT[b] if which == 0 else sinT[b]
+            pt = keep.tile([P, T], F32, name="p%d_%d%d" % (which + 1, b, h))
+            if on_gpsimd:
+                nc.gpsimd.tensor_tensor(out=pt[:], in0=qb[(b, h)][:], in1=tab[:], op=ALU.mult)
+            else:
+                nc.vector.scalar_tensor_tensor(out=pt[:], in0=qq[(b, h)][:], scalar=bias[:, h:h + 1], in1=tab[:],
+                                               op0=ALU.add, op1=ALU.mult)
+            old = pp.get((b, h, 0), (None, None))
+            pp[(b, h, 0)] = (pt, old[1]) if which == 0 else (old[0], pt)
 
         def turn_out(b, h, t0, t1):
             p1, p2 = pp[(b, h, t0)]
@@ -275,16 +300,16 @@ def tile_attentionmodule_pa_kernel(tc, x_bytes, x_scale, x_mask, Wq, bq, out):
         sm = ps_t.tile([P, 8], F32, name="sm", tag="tr")
         nc.tensor.matmul(out=sm[:, 0:B], lhsT=ones[:], rhs=msum[:], start=True, stop=True)
         rlen = keep.tile([P, B], F32, name="rlen")
+        nc.vector.reciprocal(out=rlen[:], in_=sm[:, 0:B])
         widen(0, 0, 0, True)
         widen(0, 0, 2, False)
-        nc.vector.reciprocal(out=rlen[:], in_=sm[:, 0:B])
+        nc.vector.tensor_scalar(out=step[:], in0=rlen[:], scalar1=turns[:, 0:1], scalar2=None, op0=ALU.mult)
         widen(0, 0, 1, True)
         widen(0, 0, 3, False)
-        nc.vector.tensor_scalar(out=step[:], in0=rlen[:], scalar1=turns[:, 0:1], scalar2=None, op0=ALU.mult)
-        widen(0, 1, 0, True)
-        widen(0, 1, 2, False)
         whole_turns(0)
-        widen(0, 1, 1, True)
+        widen(0, 1, 0, True)
+        widen(0, 1, 1, False)
+        widen(0, 1, 2, False)
         widen(0, 1, 3, False)
         rest_turns(0)
         dup(0)
@@ -306,10 +331,9 @@ def tile_attentionmodule_pa_kernel(tc, x_bytes, x_scale, x_mask, Wq, bq, out):
         evac_w(3)
         quant_w(0)
         project(0, 0, (0,))
-        project(0, 1, (0,))
         quant_x(0, 1)
         project(0, 0, (1,))
-        project(0, 1, (1,))
+        project(0, 1)
         sine(0, "c")
         sine(0, "s")
         rest_turns(1)

@@ -323,11 +323,13 @@ def tile_attentionmodule_pa_kernel(tc, x_bytes, x_scale, x_mask, Wq, bq, out):
         whole_turns(1)
         evac_w(0)
         evac_w(1)
-        widen(1, 0, 0, False)
+        widen(1, 0, 2, False)
         interleave(0, 1)
+        widen(1, 0, 0, True)
         evac_w(2)
-        widen(1, 0, 1, False)
+        widen(1, 1, 0, False)
         quant_x(0, 0)
+        widen(1, 0, 1, True)
         evac_w(3)
         quant_w(0)
         project(0, 0, (0,))
@@ -341,10 +343,9 @@ def tile_attentionmodule_pa_kernel(tc, x_bytes, x_scale, x_mask, Wq, bq, out):
         quant_w(1)
         project(0, 2)
         project(0, 3)
-        widen(1, 0, 2, False)
         widen(1, 0, 3, False)
         interleave(1, 0, on_gpsimd=True)
-        for j in range(J):
+        for j in range(1, J):
             widen(1, 1, j, False)
         interleave(1, 1, on_scalar=True, n0=0, n1=320)
         for h in range(H - 1):

@@ -213,14 +213,15 @@ def tile_attentionmodule_pa_kernel(tc, x_bytes, x_scale, x_mask, Wq, bq, out):
             sel = sel_cos if which == "c" else sel_sin
             nc.tensor.matmul(out=arg[(b, which)][:], lhsT=sel[:], rhs=fr[b][:], start=True, stop=True)
 
+        tabs = {}
+
         def sine(b, which):
-            tab = keep.tile([P, T], F32, name="tab%d%s" % (b, which))
+            if b not in tabs:
+                tabs[b] = keep.tile([P, 2, T], F32, name="tabs%d" % b)
             if which == "c":
-                nc.scalar.activation(out=tab[:], in_=arg[(b, which)][:], func=ACT.Sin, scale=TWO_PI, bias=halfpi[:, 0:1])
-                cosT[b] = tab
+                nc.scalar.activation(out=tabs[b][:, 0, :], in_=arg[(b, which)][:], func=ACT.Sin, scale=TWO_PI, bias=halfpi[:, 0:1])
             else:
-                nc.scalar.activation(out=tab[:], in_=arg[(b, which)][:], func=ACT.Sin, scale=sgn[:, 0:1])
-                sinT[b] = tab
+                nc.scalar.activation(out=tabs[b][:, 1, :], in_=arg[(b, which)][:], func=ACT.Sin, scale=sgn[:, 0:1])
 
         bias = keep.tile([P, H], F32, name="bias")
         qq, pp, ot, ob = {}, {}, {}, {}
@@ -242,13 +243,11 @@ def tile_attentionmodule_pa_kernel(tc, x_bytes, x_scale, x_mask, Wq, bq, out):
 
         def products(b, h, t0, t1):
             cols = slice(t0 * P, t1 * P)
-            p1 = work.tile([P, (t1 - t0) * P], F32, name="p1_%d%d%d" % (b, h, t0), tag="p1")
-            nc.vector.scalar_tensor_tensor(out=p1[:], in0=qq[(b, h)][:, cols], scalar=bias[:, h:h + 1],
-                                           in1=cosT[b][:, cols], op0=ALU.add, op1=ALU.mult)
-            p2 = work.tile([P, (t1 - t0) * P], F32, name="p2_%d%d%d" % (b, h, t0), tag="p2")
-            nc.vector.scalar_tensor_tensor(out=p2[:], in0=qq[(b, h)][:, cols], scalar=bias[:, h:h + 1],
-                                           in1=sinT[b][:, cols], op0=ALU.add, op1=ALU.mult)
-            pp[(b, h, t0)] = (p1, p2)
+            n = (t1 - t0) * P
+            both = work.tile([P, 2, n], F32, name="pp_%d%d%d" % (b, h, t0), tag="pp")
+            nc.vector.scalar_tensor_tensor(out=both[:], in0=qq[(b, h)][:, cols].rearrange("p (o n) -> p o n", o=1).to_broadcast([P, 2, n]),
+                                           scalar=bias[:, h:h + 1], in1=tabs[b][:, :, cols], op0=ALU.add, op1=ALU.mult)
+            pp[(b, h, t0)] = (both[:, 0, :], both[:, 1, :])
 
         qb = {}
 
@@ -327,12 +326,13 @@ def tile_attentionmodule_pa_kernel(tc, x_bytes, x_scale, x_mask, Wq, bq, out):
         interleave(0, 1)
         widen(1, 0, 0, True)
         evac_w(2)
-        widen(1, 1, 0, False)
+        widen(1, 0, 3, False)
         quant_x(0, 0)
-        widen(1, 0, 1, True)
+        widen(1, 1, 0, True)
         evac_w(3)
         quant_w(0)
         project(0, 0, (0,))
+        widen(1, 1, 1, True)
         quant_x(0, 1)
         project(0, 0, (1,))
         project(0, 1)
@@ -343,11 +343,11 @@ def tile_attentionmodule_pa_kernel(tc, x_bytes, x_scale, x_mask, Wq, bq, out):
         quant_w(1)
         project(0, 2)
         project(0, 3)
-        widen(1, 0, 3, False)
+        widen(1, 0, 1, True)
         interleave(1, 0, on_gpsimd=True)
-        for j in range(1, J):
-            widen(1, 1, j, False)
-        interleave(1, 1, on_scalar=True, n0=0, n1=320)
+        widen(1, 1, 2, False)
+        widen(1, 1, 3, False)
+        interleave(1, 1, on_scalar=True, n0=0, n1=T)
         for h in range(H - 1):
             products(0, h, 0, TB)
             turn_out(0, h, 0, TB)
@@ -355,7 +355,6 @@ def tile_attentionmodule_pa_kernel(tc, x_bytes, x_scale, x_mask, Wq, bq, out):
         sine(1, "s")
         quant_x(1, 0)
         project(1, 0, (0,))
-        interleave(1, 1, n0=320, n1=T)
         for h in range(H - 1):
             evac_out(0, h, 0, TB)
         quant_x(1, 1)

@@ -69,8 +69,10 @@ def tile_attentionmodule_pa_kernel(tc, x_bytes, x_scale, x_mask, Wq, bq, out):
         nc.scalar.dma_start(out=zb[0:H, :], in_=bq.rearrange("(h m) -> h m", m=P))
         warm = keep.tile([P, 1], F32, name="warm")
         nc.scalar.activation(out=warm[:], in_=zero1[:], func=ACT.Sin)
-        load_x(0, 0)
+        x00 = x_bytes[0].rearrange("(g p j) n -> g p j n", p=P, j=J)[0]
+        nc.sync.dma_start(out=xb[(0, 0)][:, 0:J:2, :], in_=x00[:, 0:J:2, :])
         nc.sync.dma_start(out=xs[:], in_=x_scale.rearrange("o (g p j) q -> p (o g) (j q)", p=P, j=J))
+        nc.sync.dma_start(out=xb[(0, 0)][:, 1:J:2, :], in_=x00[:, 1:J:2, :])
         load_x(0, 1)
         load_w(0)
         load_w(1)

@@ -1,7 +1,6 @@
 from contextlib import ExitStack
 
 import concourse.mybir as mybir
-from concourse.masks import make_identity
 
 B, T, DM, A, H = 2, 512, 1024, 512, 4
 HD = A // H
@@ -76,19 +75,19 @@ def tile_attentionmodule_pa_kernel(tc, x_bytes, x_scale, x_mask, Wq, bq, out):
         load_x(0, 1)
         load_w(0)
         load_w(1)
+        load_x(1, 0)
         load_w(2)
         load_w(3)
-        load_x(1, 0)
         load_x(1, 1)
 
         pidx_i = keep.tile([P, 1], I32, name="pidx_i")
         nc.gpsimd.iota(pidx_i[:], pattern=[[0, 1]], base=0, channel_multiplier=1)
+        tpos_i = keep.tile([P, T], I32, name="tpos_i")
+        nc.gpsimd.iota(tpos_i[:], pattern=[[1, T]], base=0, channel_multiplier=0)
         ones = keep.tile([P, P], BF16, name="ones")
         nc.vector.memset(ones[:], 1.0)
-        pidx = keep.tile([P, 1], F32, name="pidx")
-        nc.vector.tensor_copy(out=pidx[:], in_=pidx_i[:])
         upper = keep.tile([P, 1], F32, name="upper")
-        nc.vector.tensor_scalar(out=upper[:], in0=pidx[:], scalar1=64.0, scalar2=None, op0=ALU.is_ge)
+        nc.vector.tensor_scalar(out=upper[:], in0=pidx_i[:], scalar1=64, scalar2=None, op0=ALU.is_ge)
         bits = keep.tile([P, 6], I32, name="bits")
         facs = keep.tile([P, 6], F32, name="facs")
         for k in range(6):
@@ -99,10 +98,14 @@ def tile_attentionmodule_pa_kernel(tc, x_bytes, x_scale, x_mask, Wq, bq, out):
             ratio = 10000.0 ** (-(2.0 ** k) / 64.0)
             nc.vector.tensor_scalar(out=facs[:, k:k + 1], in0=bits[:, k:k + 1], scalar1=(ratio - 1.0) * lead,
                                     scalar2=lead, op0=ALU.mult, op1=ALU.add)
+        partner = keep.tile([P, 1], I32, name="partner")
+        nc.vector.tensor_scalar(out=partner[:], in0=pidx_i[:], scalar1=64, scalar2=None, op0=ALU.bitwise_xor)
         ident = keep.tile([P, P], F32, name="ident")
-        make_identity(nc, ident[:])
-        tpos_i = keep.tile([P, T], I32, name="tpos_i")
-        nc.gpsimd.iota(tpos_i[:], pattern=[[1, T]], base=0, channel_multiplier=0)
+        nc.vector.tensor_scalar(out=ident[:], in0=tpos_i[:, 0:P], scalar1=pidx_i[:, 0:1], scalar2=None, op0=ALU.is_equal)
+        tpos = keep.tile([P, T], F32, name="tpos")
+        nc.vector.tensor_copy(out=tpos[:], in_=tpos_i[:])
+        swap = keep.tile([P, P], F32, name="swap")
+        nc.vector.tensor_scalar(out=swap[:], in0=tpos_i[:, 0:P], scalar1=partner[:, 0:1], scalar2=None, op0=ALU.is_equal)
         sgn = keep.tile([P, 1], F32, name="sgn")
         nc.vector.tensor_scalar(out=sgn[:], in0=upper[:], scalar1=-2.0 * TWO_PI, scalar2=TWO_PI,
                                 op0=ALU.mult, op1=ALU.add)
@@ -110,28 +113,10 @@ def tile_attentionmodule_pa_kernel(tc, x_bytes, x_scale, x_mask, Wq, bq, out):
         nc.vector.tensor_scalar(out=quarter[:], in0=upper[:], scalar1=0.25, scalar2=None, op0=ALU.mult)
         halfpi = keep.tile([P, 1], F32, name="halfpi")
         nc.vector.tensor_scalar(out=halfpi[:], in0=upper[:], scalar1=0.0, scalar2=TWO_PI / 4.0, op0=ALU.mult, op1=ALU.add)
+        first4 = keep.tile([P, H], BF16, name="first4")
+        nc.vector.tensor_copy(out=first4[:], in_=ident[:, 0:H])
         turns = keep.tile([P, 1], F32, name="turns")
         nc.vector.tensor_reduce(out=turns[:], in_=facs[:], axis=AX.X, op=ALU.mult)
-        tpos = keep.tile([P, T], F32, name="tpos")
-        swap = keep.tile([P, P], F32, name="swap")
-        sel_sin = keep.tile([P, P], F32, name="sel_sin")
-        sel_cos = keep.tile([P, P], F32, name="sel_cos")
-        first4 = keep.tile([P, H], BF16, name="first4")
-
-        def selectors():
-            nc.vector.tensor_copy(out=first4[:], in_=ident[:, 0:H])
-            nc.vector.tensor_copy(out=sel_cos[:, 0:64], in_=ident[:, 64:128])
-            nc.vector.tensor_copy(out=sel_cos[:, 64:128], in_=ident[:, 64:128])
-            nc.vector.tensor_copy(out=sel_sin[:, 0:64], in_=ident[:, 0:64])
-            nc.vector.tensor_copy(out=sel_sin[:, 64:128], in_=ident[:, 0:64])
-
-        def swapper():
-            nc.vector.tensor_copy(out=swap[:, 0:64], in_=ident[:, 64:128])
-            nc.vector.tensor_copy(out=swap[:, 64:128], in_=ident[:, 0:64])
-
-        selectors()
-        swapper()
-        nc.vector.tensor_copy(out=tpos[:], in_=tpos_i[:])
 
         def widen(b, g, j, on_vector):
             src = xb[(b, g)][:, j, :].bitcast(FP8)
@@ -205,15 +190,10 @@ def tile_attentionmodule_pa_kernel(tc, x_bytes, x_scale, x_mask, Wq, bq, out):
                                            op0=ALU.mult, op1=ALU.subtract)
 
         def dup(b):
-            for which, lo in (("s", 0), ("c", 64)):
+            for which, lo in (("c", 64), ("s", 0)):
                 arg[(b, which)] = keep.tile([P, T], F32, name="arg%d%s" % (b, which))
                 nc.sync.dma_start(out=arg[(b, which)][0:64, :], in_=fr[b][lo:lo + 64, :])
                 nc.sync.dma_start(out=arg[(b, which)][64:128, :], in_=fr[b][lo:lo + 64, :])
-
-        def spread(b, which):
-            arg[(b, which)] = ps_t.tile([P, T], F32, name="arg%d%s" % (b, which), tag="tr")
-            sel = sel_cos if which == "c" else sel_sin
-            nc.tensor.matmul(out=arg[(b, which)][:], lhsT=sel[:], rhs=fr[b][:], start=True, stop=True)
 
         tabs = {}
 

from contextlib import ExitStack

import concourse.mybir as mybir

B, T, DM, A, H = 2, 512, 1024, 512, 4
HD = A // H
FLOPS = 2 * B * T * DM * A

F32 = mybir.dt.float32
BF16 = mybir.dt.bfloat16
U8 = mybir.dt.uint8
U32 = mybir.dt.uint32
I32 = mybir.dt.int32
FP8 = mybir.dt.float8_e4m3fn
FP8X4 = mybir.dt.float8_e4m3fn_x4
ALU = mybir.AluOpType
ACT = mybir.ActivationFunctionType
AX = mybir.AxisListType

P = 128
J = 4
G = DM // (P * J)
TB = T // P
TWO_PI = 6.283185307179586


def tile_attentionmodule_pa_kernel(tc, x_bytes, x_scale, x_mask, Wq, bq, out):
    nc = tc.nc
    with ExitStack() as ctx:
        keep = ctx.enter_context(tc.tile_pool(name="keep", bufs=1))
        work = ctx.enter_context(tc.tile_pool(name="work", bufs=4))
        ps_q = ctx.enter_context(tc.psum_pool(name="ps_q", bufs=1))
        ps_t = ctx.enter_context(tc.psum_pool(name="ps_t", bufs=4))
        ctx.enter_context(tc.manual_schedule())

        xs = keep.tile([P, G, J], F32, name="xs")
        mk = keep.tile([P, B, 4], BF16, name="mk")
        zb = keep.tile([P, P], BF16, name="zb")
        xb, xw, xi, xc, xsc = {}, {}, {}, {}, {}
        for b in range(B):
            for g in range(G):
                xb[(b, g)] = keep.tile([P, J, T], U8, name="xb%d%d" % (b, g))
                xw[(b, g)] = keep.tile([P, J, T], BF16, name="xw%d%d" % (b, g))
                xi[(b, g)] = keep.tile([P, T, J], BF16, name="xi%d%d" % (b, g), align_bytes=64)
                xc[(b, g)] = keep.tile([P, T], U32, name="xc%d%d" % (b, g), align_bytes=64)
                xsc[(b, g)] = keep.tile([P, T], U8, name="xsc%d%d" % (b, g), align_bytes=64)
        wraw, wi, wc, wsc = [], [], [], []
        for r in range(H):
            wraw.append(keep.tile([P, DM], BF16, name="wraw%d" % r))
        for rp in range(H // 2):
            wi.append(keep.tile([P, 2, G * P * J], BF16, name="wi%d" % rp, align_bytes=64))
            wc.append(keep.tile([P, 2, G * P], U32, name="wc%d" % rp, align_bytes=64))
            wsc.append(keep.tile([P, 2, G * P], U8, name="wsc%d" % rp, align_bytes=64))

        def load_x(b, g):
            nc.sync.dma_start(
                out=xb[(b, g)][:],
                in_=x_bytes[b].rearrange("(g p j) n -> g p j n", p=P, j=J)[g],
            )

        def load_w(r):
            nc.sync.dma_start(out=wraw[r][:], in_=Wq[r * P:(r + 1) * P, :])

        nc.scalar.dma_start(out=mk[:], in_=x_mask.rearrange("b o (p j) -> p (b o) j", j=4))
        nc.vector.memset(zb[:], 0.0)
        zero1 = keep.tile([P, 1], F32, name="zero1")
        nc.vector.memset(zero1[:], 0.0)
        nc.scalar.dma_start(out=zb[0:H, :], in_=bq.rearrange("(h m) -> h m", m=P))
        warm = keep.tile([P, 1], F32, name="warm")
        nc.scalar.activation(out=warm[:], in_=zero1[:], func=ACT.Sin)
        x00 = x_bytes[0].rearrange("(g p j) n -> g p j n", p=P, j=J)[0]
        nc.sync.dma_start(out=xb[(0, 0)][:, 0:J:2, :], in_=x00[:, 0:J:2, :])
        nc.sync.dma_start(out=xs[:], in_=x_scale.rearrange("o (g p j) q -> p (o g) (j q)", p=P, j=J))
        nc.sync.dma_start(out=xb[(0, 0)][:, 1:J:2, :], in_=x00[:, 1:J:2, :])
        load_x(0, 1)
        load_w(0)
        load_w(1)
        load_x(1, 0)
        load_w(2)
        load_w(3)
        load_x(1, 1)

        pidx_i = keep.tile([P, 1], I32, name="pidx_i")
        nc.gpsimd.iota(pidx_i[:], pattern=[[0, 1]], base=0, channel_multiplier=1)
        tpos_i = keep.tile([P, T], I32, name="tpos_i")
        nc.gpsimd.iota(tpos_i[:], pattern=[[1, T]], base=0, channel_multiplier=0)
        ones = keep.tile([P, P], BF16, name="ones")
        nc.vector.memset(ones[:], 1.0)
        upper = keep.tile([P, 1], F32, name="upper")
        nc.vector.tensor_scalar(out=upper[:], in0=pidx_i[:], scalar1=64, scalar2=None, op0=ALU.is_ge)
        bits = keep.tile([P, 6], I32, name="bits")
        facs = keep.tile([P, 6], F32, name="facs")
        for k in range(6):
            nc.vector.tensor_scalar(out=bits[:, k:k + 1], in0=pidx_i[:], scalar1=k, scalar2=1,
                                    op0=ALU.logical_shift_right, op1=ALU.bitwise_and)
        for k in range(6):
            lead = 10.0 / TWO_PI if k == 0 else 1.0
            ratio = 10000.0 ** (-(2.0 ** k) / 64.0)
            nc.vector.tensor_scalar(out=facs[:, k:k + 1], in0=bits[:, k:k + 1], scalar1=(ratio - 1.0) * lead,
                                    scalar2=lead, op0=ALU.mult, op1=ALU.add)
        partner = keep.tile([P, 1], I32, name="partner")
        nc.vector.tensor_scalar(out=partner[:], in0=pidx_i[:], scalar1=64, scalar2=None, op0=ALU.bitwise_xor)
        ident = keep.tile([P, P], F32, name="ident")
        nc.vector.tensor_scalar(out=ident[:], in0=tpos_i[:, 0:P], scalar1=pidx_i[:, 0:1], scalar2=None, op0=ALU.is_equal)
        tpos = keep.tile([P, T], F32, name="tpos")
        nc.vector.tensor_copy(out=tpos[:], in_=tpos_i[:])
        swap = keep.tile([P, P], F32, name="swap")
        nc.vector.tensor_scalar(out=swap[:], in0=tpos_i[:, 0:P], scalar1=partner[:, 0:1], scalar2=None, op0=ALU.is_equal)
        sgn = keep.tile([P, 1], F32, name="sgn")
        nc.vector.tensor_scalar(out=sgn[:], in0=upper[:], scalar1=-2.0 * TWO_PI, scalar2=TWO_PI,
                                op0=ALU.mult, op1=ALU.add)
        quarter = keep.tile([P, 1], F32, name="quarter")
        nc.vector.tensor_scalar(out=quarter[:], in0=upper[:], scalar1=0.25, scalar2=None, op0=ALU.mult)
        halfpi = keep.tile([P, 1], F32, name="halfpi")
        nc.vector.tensor_scalar(out=halfpi[:], in0=upper[:], scalar1=0.0, scalar2=TWO_PI / 4.0, op0=ALU.mult, op1=ALU.add)
        first4 = keep.tile([P, H], BF16, name="first4")
        nc.vector.tensor_copy(out=first4[:], in_=ident[:, 0:H])
        turns = keep.tile([P, 1], F32, name="turns")
        nc.vector.tensor_reduce(out=turns[:], in_=facs[:], axis=AX.X, op=ALU.mult)

        def widen(b, g, j, on_vector):
            src = xb[(b, g)][:, j, :].bitcast(FP8)
            dst = xw[(b, g)][:, j, :]
            if on_vector:
                nc.vector.tensor_scalar(out=dst, in0=src, scalar1=xs[:, g, j:j + 1], scalar2=None, op0=ALU.mult)
            else:
                nc.scalar.activation(out=dst, in_=src, func=ACT.Copy, scale=xs[:, g, j:j + 1])

        def interleave(b, g, on_gpsimd=False, n0=0, n1=T, on_scalar=False):
            if on_scalar:
                nc.scalar.copy(out=xi[(b, g)][:, n0:n1, :], in_=xw[(b, g)][:, :, n0:n1].rearrange("p j n -> p n j"))
            elif on_gpsimd:
                nc.gpsimd.tensor_scalar(out=xi[(b, g)][:, n0:n1, :], in0=xw[(b, g)][:, :, n0:n1].rearrange("p j n -> p n j"),
                                        scalar1=1.0, scalar2=0.0, op0=ALU.mult, op1=ALU.add)
            else:
                src = xw[(b, g)][:, :, n0:n1].rearrange("p j (c i) -> p c j i", i=4)
                dst = xi[(b, g)][:, n0:n1, :].rearrange("p (c i) j -> p c j i", i=4)
                nc.vector.tensor_copy(out=dst, in_=src)

        def quant_x(b, g):
            nc.vector.quantize_mx(
                out=xc[(b, g)][:].bitcast(FP8X4),
                scales=xsc[(b, g)][:],
                in_=xi[(b, g)][:].rearrange("p n j -> p (n j)"),
            )

        wt = {}

        def turn_w(r):
            words = wraw[r][:].bitcast(F32)
            wt[r] = ps_t.tile([P, G, 2, P], F32, name="wt%d" % r, tag="tr")
            for g in range(G):
                for u in range(2):
                    nc.tensor.transpose(wt[r][:, g, u, :], words[:, 256 * g + u:256 * (g + 1):2], ident[:])

        def evac_w(r):
            dst = wi[r // 2][:, r % 2, :].bitcast(F32).rearrange("p (g a u) -> p g a u", g=G, u=2)
            nc.scalar.copy(out=dst, in_=wt[r][:].rearrange("p g u a -> p g a u"))

        def quant_w(rp):
            nc.vector.quantize_mx(
                out=wc[rp][:].rearrange("p r c -> p (r c)").bitcast(FP8X4),
                scales=wsc[rp][:].rearrange("p r c -> p (r c)"),
                in_=wi[rp][:].rearrange("p r c -> p (r c)"),
            )

        step = keep.tile([P, B], F32, name="step")
        vv, nn, fr, arg, cosT, sinT = {}, {}, {}, {}, {}, {}

        def turns_of(b):
            vv[b] = keep.tile([P, T], F32, name="vv%d" % b)
            nc.gpsimd.tensor_scalar(out=vv[b][:], in0=tpos[:], scalar1=step[:, b:b + 1], scalar2=quarter[:, 0:1],
                                    op0=ALU.mult, op1=ALU.add)
            nn[b] = keep.tile([P, T], I32, name="nn%d" % b)
            nc.gpsimd.tensor_scalar(out=nn[b][:], in0=vv[b][:], scalar1=1.0, scalar2=0.0,
                                    op0=ALU.mult, op1=ALU.add)

        def frac_of(b):
            fr[b] = keep.tile([P, T], F32, name="fr%d" % b)
            nc.vector.tensor_tensor(out=fr[b][:], in0=vv[b][:], in1=nn[b][:], op=ALU.subtract)

        def whole_turns(b):
            nn[b] = keep.tile([P, T], I32, name="nn%d" % b)
            nc.vector.tensor_scalar(out=nn[b][:], in0=tpos[:], scalar1=step[:, b:b + 1], scalar2=quarter[:, 0:1],
                                    op0=ALU.mult, op1=ALU.add)

        def rest_turns(b):
            fr[b] = keep.tile([P, T], F32, name="fr%d" % b)
            nc.vector.scalar_tensor_tensor(out=fr[b][:], in0=tpos[:], scalar=step[:, b:b + 1], in1=nn[b][:],
                                           op0=ALU.mult, op1=ALU.subtract)

        def dup(b):
            for which, lo in (("c", 64), ("s", 0)):
                arg[(b, which)] = keep.tile([P, T], F32, name="arg%d%s" % (b, which))
                nc.sync.dma_start(out=arg[(b, which)][0:64, :], in_=fr[b][lo:lo + 64, :])
                nc.sync.dma_start(out=arg[(b, which)][64:128, :], in_=fr[b][lo:lo + 64, :])

        tabs = {}

        def sine(b, which):
            if b not in tabs:
                tabs[b] = keep.tile([P, 2, T], F32, name="tabs%d" % b)
            if which == "c":
                nc.scalar.activation(out=tabs[b][:, 0, :], in_=arg[(b, which)][:], func=ACT.Sin, scale=TWO_PI, bias=halfpi[:, 0:1])
            else:
                nc.scalar.activation(out=tabs[b][:, 1, :], in_=arg[(b, which)][:], func=ACT.Sin, scale=sgn[:, 0:1])

        bias = keep.tile([P, H], F32, name="bias")
        qq, pp, ot, ob = {}, {}, {}, {}

        def project(b, h, passes=(0, 1), bank=None):
            if passes[0] == 0:
                qq[(b, h)] = ps_q.tile([P, T], F32, name="q%d%d" % (b, h), tag="q%d" % (h if bank is None else bank))
            for g in passes:
                cols = slice(g * P, (g + 1) * P)
                nc.tensor.matmul_mx(
                    out=qq[(b, h)][:],
                    lhsT=wc[h // 2][:, h % 2, cols].bitcast(FP8X4),
                    lhsT_scale=wsc[h // 2][:, h % 2, cols],
                    rhs=xc[(b, g)][:].bitcast(FP8X4),
                    rhs_scale=xsc[(b, g)][:],
                    start=(g == 0),
                    stop=(g == G - 1),
                )

        def products(b, h, t0, t1):
            cols = slice(t0 * P, t1 * P)
            n = (t1 - t0) * P
            both = work.tile([P, 2, n], F32, name="pp_%d%d%d" % (b, h, t0), tag="pp")
            nc.vector.scalar_tensor_tensor(out=both[:], in0=qq[(b, h)][:, cols].rearrange("p (o n) -> p o n", o=1).to_broadcast([P, 2, n]),
                                           scalar=bias[:, h:h + 1], in1=tabs[b][:, :, cols], op0=ALU.add, op1=ALU.mult)
            pp[(b, h, t0)] = (both[:, 0, :], both[:, 1, :])

        qb = {}

        def evac_q(b, h):
            qb[(b, h)] = keep.tile([P, T], F32, name="qb%d%d" % (b, h))
            nc.scalar.activation(out=qb[(b, h)][:], in_=qq[(b, h)][:], func=ACT.Identity, bias=bias[:, h:h + 1])

        def products_g(b, h, t0, t1):
            cols = slice(t0 * P, t1 * P)
            p1 = keep.tile([P, (t1 - t0) * P], F32, name="p1_%d%d%d" % (b, h, t0))
            nc.gpsimd.tensor_tensor(out=p1[:], in0=qb[(b, h)][:, cols], in1=cosT[b][:, cols], op=ALU.mult)
            p2 = keep.tile([P, (t1 - t0) * P], F32, name="p2_%d%d%d" % (b, h, t0))
            nc.gpsimd.tensor_tensor(out=p2[:], in0=qb[(b, h)][:, cols], in1=sinT[b][:, cols], op=ALU.mult)
            pp[(b, h, t0)] = (p1, p2)

        def product(b, h, which, on_gpsimd=False):
            tab = cosT[b] if which == 0 else sinT[b]
            pt = keep.tile([P, T], F32, name="p%d_%d%d" % (which + 1, b, h))
            if on_gpsimd:
                nc.gpsimd.tensor_tensor(out=pt[:], in0=qb[(b, h)][:], in1=tab[:], op=ALU.mult)
            else:
                nc.vector.scalar_tensor_tensor(out=pt[:], in0=qq[(b, h)][:], scalar=bias[:, h:h + 1], in1=tab[:],
                                               op0=ALU.add, op1=ALU.mult)
            old = pp.get((b, h, 0), (None, None))
            pp[(b, h, 0)] = (pt, old[1]) if which == 0 else (old[0], pt)

        def turn_out(b, h, t0, t1):
            p1, p2 = pp[(b, h, t0)]
            o = ps_t.tile([P, t1 - t0, P], F32, name="ot%d%d%d" % (b, h, t0), tag="tr")
            for tb in range(t1 - t0):
                cols = slice(tb * P, (tb + 1) * P)
                nc.tensor.matmul(out=o[:, tb, :], lhsT=p1[:, cols], rhs=ident[:], is_transpose=True,
                                 start=True, stop=False)
                nc.tensor.matmul(out=o[:, tb, :], lhsT=p2[:, cols], rhs=swap[:], is_transpose=True,
                                 start=False, stop=True)
            ot[(b, h, t0)] = o

        def evac_out(b, h, t0, t1, on_vector=False, queue=None):
            o = keep.tile([P, t1 - t0, P], F32, name="ob%d%d%d" % (b, h, t0))
            if on_vector:
                nc.vector.tensor_copy(out=o[:], in_=ot[(b, h, t0)][:])
            else:
                nc.scalar.copy(out=o[:], in_=ot[(b, h, t0)][:])
            (queue or nc.sync).dma_start(out=out[h, b].rearrange("(tb p) d -> p tb d", p=P)[:, t0:t1, :], in_=o[:])

        msum = keep.tile([P, B], BF16, name="msum")
        with nc.allow_low_precision("sums of four ones or zeros are exact in bfloat16"):
            nc.vector.tensor_reduce(out=msum[:], in_=mk[:], axis=AX.X, op=ALU.add)
        sm = ps_t.tile([P, 8], F32, name="sm", tag="tr")
        nc.tensor.matmul(out=sm[:, 0:B], lhsT=ones[:], rhs=msum[:], start=True, stop=True)
        rlen = keep.tile([P, B], F32, name="rlen")
        nc.vector.reciprocal(out=rlen[:], in_=sm[:, 0:B])
        widen(0, 0, 0, True)
        widen(0, 0, 2, False)
        nc.vector.tensor_scalar(out=step[:], in0=rlen[:], scalar1=turns[:, 0:1], scalar2=None, op0=ALU.mult)
        widen(0, 0, 1, True)
        widen(0, 0, 3, False)
        whole_turns(0)
        widen(0, 1, 0, True)
        widen(0, 1, 1, False)
        widen(0, 1, 2, False)
        widen(0, 1, 3, False)
        rest_turns(0)
        dup(0)
        nc.tensor.matmul(out=sm[:, 4:4 + H], lhsT=zb[:], rhs=first4[:], start=True, stop=True)
        turn_w(0)
        turn_w(1)
        turn_w(2)
        interleave(0, 0)
        nc.vector.tensor_copy(out=bias[:], in_=sm[:, 4:4 + H])
        turn_w(3)
        whole_turns(1)
        evac_w(0)
        evac_w(1)
        widen(1, 0, 2, False)
        interleave(0, 1)
        widen(1, 0, 0, True)
        evac_w(2)
        widen(1, 0, 3, False)
        quant_x(0, 0)
        widen(1, 1, 0, True)
        evac_w(3)
        quant_w(0)
        project(0, 0, (0,))
        widen(1, 1, 1, True)
        quant_x(0, 1)
        project(0, 0, (1,))
        project(0, 1)
        sine(0, "c")
        sine(0, "s")
        rest_turns(1)
        dup(1)
        quant_w(1)
        project(0, 2)
        project(0, 3)
        widen(1, 0, 1, True)
        interleave(1, 0, on_gpsimd=True)
        widen(1, 1, 2, False)
        widen(1, 1, 3, False)
        interleave(1, 1, on_scalar=True, n0=0, n1=T)
        for h in range(H - 1):
            products(0, h, 0, TB)
            turn_out(0, h, 0, TB)
        sine(1, "c")
        sine(1, "s")
        quant_x(1, 0)
        project(1, 0, (0,))
        for h in range(H - 1):
            evac_out(0, h, 0, TB)
        quant_x(1, 1)
        project(1, 0, (1,))
        project(1, 1)
        project(1, 2)
        products(0, 3, 0, TB)
        turn_out(0, 3, 0, TB)
        evac_out(0, 3, 0, TB)
        project(1, 3)
        for h in range(H - 1):
            products(1, h, 0, TB)
            turn_out(1, h, 0, TB)
            evac_out(1, h, 0, TB)
        products(1, 3, 0, 2)
        turn_out(1, 3, 0, 2)
        evac_out(1, 3, 0, 2)
        products(1, 3, 2, 4)
        turn_out(1, 3, 2, 4)
        evac_out(1, 3, 2, 4, queue=nc.scalar)
